import numpy as np
import ml_dtypes


def mxq(x, axis, fmt="e4m3"):
    dtype, down = {"e4m3": (ml_dtypes.float8_e4m3fn, 7), "e5m2": (ml_dtypes.float8_e5m2, 14)}[fmt]
    v = np.moveaxis(np.asarray(x, np.float32).astype(ml_dtypes.bfloat16).astype(np.float64), axis, -1)
    blocks = v.reshape(v.shape[:-1] + (-1, 32))
    amax = np.abs(blocks).max(-1, keepdims=True)
    byte = np.maximum(np.where(amax > 0, np.frexp(amax)[1] - 1 + 127, 0) - down, 1)
    scale = np.exp2(byte - 127.0)
    codes = (blocks / scale).astype(np.float32).astype(dtype).astype(np.float64)
    return np.moveaxis((codes * scale).reshape(v.shape), -1, axis)


WIDE = False


def mx_kscale(k):
    if not WIDE:
        return np.ones(k)
    levels = np.array([10, -10, 5, -5, 0])
    a = np.random.permutation(np.resize(levels, k // 512 * 4)).reshape(k // 512, 4)
    idx = np.arange(k)
    return np.exp2(a[idx // 512, idx % 128 // 32])


BF16 = ml_dtypes.bfloat16


def bf(x):
    return np.asarray(x, np.float32).astype(BF16)


def f64(x):
    return np.asarray(x).astype(np.float64)


B, E, M, NH, NKV, HD, D = 2, 64, 512, 8, 4, 128, 512
G = NH // NKV
A = NH * HD
SCALE = 0.5
QK = 2.0 / HD ** 0.25


def setup_inputs():
    t = mx_kscale(A).reshape(NKV, G, HD)[:, 0, :]
    tq = np.repeat(t, G, axis=0).reshape(A)
    sgn = np.where(np.random.standard_normal((NKV, HD)) > 0.0, 1.0, -1.0)
    v = sgn * (2.0 + 1.5 * np.random.uniform(-1.0, 1.0, (B, M, NKV, HD)))
    return {"q_pos": bf(np.random.standard_normal((E, NH, HD)) * QK),
            "k_mem": bf(np.random.standard_normal((B, M, NKV, HD)) * QK),
            "v_mem": bf(v * t),
            "Wo": bf(np.random.standard_normal((D, A)) / np.sqrt(A) / tq)}


def reference(q_pos, k_mem, v_mem, Wo):
    q = f64(q_pos).transpose(1, 0, 2).reshape(NKV, G * E, HD)
    kt = f64(k_mem).transpose(0, 2, 3, 1)
    v = f64(v_mem).transpose(0, 2, 1, 3)
    s = (q @ kt) * SCALE
    e = np.exp(s - s.max(-1, keepdims=True))
    o = (mxq(e, 3, "e4m3") @ mxq(v, 2, "e4m3")) / e.sum(-1, keepdims=True)
    a = o.reshape(B, NKV, G, E, HD).transpose(0, 3, 1, 2, 4).reshape(B, E, A)
    return mxq(a, 2, "e4m3") @ mxq(f64(Wo).T, 0, "e4m3")

@@ -1,0 +1,264 @@
+from contextlib import ExitStack
+
+import concourse.masks as masks
+import concourse.mybir as mybir
+
+F32 = mybir.dt.float32
+BF16 = mybir.dt.bfloat16
+U32 = mybir.dt.uint32
+U8 = mybir.dt.uint8
+FP8X4 = mybir.dt.float8_e4m3fn_x4
+ACT = mybir.ActivationFunctionType
+ALU = mybir.AluOpType
+AXIS = mybir.AxisListType
+
+B, E, M, NH, NKV, HD, D = 2, 64, 512, 8, 4, 128, 512
+G = NH // NKV
+SCALE = 0.5
+P = 128
+PACK = 4
+UNITS = B * NKV
+PAIRS = NKV // 2
+KEYS_AHEAD = 4
+SCORES_AHEAD = 2
+
+FLOPS = 2 * B * NH * E * HD * M * 2 + 2 * B * E * NH * HD * D
+
+
+def tile_qwen2dymemdecoderlayer_pa_s_kernel(tc, q_pos, k_mem, v_mem, Wo, out):
+    nc = tc.nc
+    with ExitStack() as ctx:
+        keep = ctx.enter_context(tc.tile_pool(name="keep", bufs=1))
+        psum3 = ctx.enter_context(tc.psum_pool(name="psum3", bufs=3))
+        psum2 = ctx.enter_context(tc.psum_pool(name="psum2", bufs=2))
+        ctx.enter_context(tc.manual_schedule())
+
+        q_sb = keep.tile([P, NKV, HD], BF16, name="q_sb")
+        q_view = q_pos.rearrange("e (g j) d -> j e g d", j=G)
+        for j in range(G):
+            nc.sync.dma_start(out=q_sb[j * E : (j + 1) * E, :, :], in_=q_view[j])
+        k_sb = [keep.tile([P, PACK, NKV * HD], BF16, name="k_sb%d" % b) for b in range(B)]
+        v_sb = [keep.tile([P, PACK, NKV * HD], BF16, name="v_sb%d" % b) for b in range(B)]
+        for b in range(B):
+            nc.sync.dma_start(out=k_sb[b][:], in_=k_mem[b].rearrange("(p t) g d -> p t (g d)", t=PACK))
+        for b in range(B):
+            nc.sync.dma_start(out=v_sb[b][:], in_=v_mem[b].rearrange("(p t) g d -> p t (g d)", t=PACK))
+        wo_sb = keep.tile([P, D // P, PAIRS, G, 2, HD], BF16, name="wo_sb")
+        wo_view = Wo.rearrange("(r p) (c u j d) -> c u j p r d", p=P, c=PAIRS, u=2, j=G)
+        for c in range(PAIRS):
+            for j in range(G):
+                for u in range(2):
+                    nc.sync.dma_start(out=wo_sb[:, :, c, j, u, :], in_=wo_view[c, u, j])
+
+        ident_bf = keep.tile([P, P], BF16, name="ident_bf")
+        masks.make_identity(nc, ident_bf[:])
+        ident_f32 = keep.tile([P, P], F32, name="ident_f32")
+        masks.make_identity(nc, ident_f32[:])
+        warm = keep.tile([P, 1], F32, name="warm")
+        nc.vector.memset(warm[:], 0.0)
+        nc.scalar.activation(out=warm[:], in_=warm[:], func=ACT.Exp)
+
+        qT_sb = keep.tile([P, NKV, P], BF16, name="qT_sb")
+        kT_sb = [keep.tile([P, M], BF16, name="kT_sb%d" % n) for n in range(UNITS)]
+        e_sb = [keep.tile([P, M], BF16, name="e_sb%d" % n) for n in range(UNITS)]
+        e_grouped = [keep.tile([P, P * PACK], BF16, name="e_grouped%d" % n, align_bytes=64) for n in range(UNITS)]
+        e_codes = keep.tile([P, UNITS, P], U32, name="e_codes", align_bytes=64)
+        e_scales = keep.tile([P, UNITS, P], U8, name="e_scales", align_bytes=64)
+        neg_max = keep.tile([P, UNITS], F32, name="neg_max")
+        row_sum = keep.tile([P, UNITS], F32, name="row_sum")
+        inv_sum = keep.tile([P, UNITS], F32, name="inv_sum")
+        v_grouped = [keep.tile([P, NKV * HD * PACK], BF16, name="v_grouped%d" % b, align_bytes=64) for b in range(B)]
+        v_codes = keep.tile([P, B, NKV * HD], U32, name="v_codes", align_bytes=64)
+        v_scales = keep.tile([P, B, NKV * HD], U8, name="v_scales", align_bytes=64)
+        a_sb = [keep.tile([P, 2 * HD], BF16, name="a_sb%d" % i) for i in range(B * PAIRS)]
+        a_grouped = [keep.tile([P, B * E * PACK], BF16, name="a_grouped%d" % c, align_bytes=64) for c in range(PAIRS)]
+        a_codes = keep.tile([P, PAIRS, B * E], U32, name="a_codes", align_bytes=64)
+        a_scales = keep.tile([P, PAIRS, B * E], U8, name="a_scales", align_bytes=64)
+        w_grouped = [keep.tile([P, D * PACK], BF16, name="w_grouped%d" % c, align_bytes=64) for c in range(PAIRS)]
+        w_codes = keep.tile([P, PAIRS, D], U32, name="w_codes", align_bytes=64)
+        w_scales = keep.tile([P, PAIRS, D], U8, name="w_scales", align_bytes=64)
+        out_sb = keep.tile([P, D], F32, name="out_sb")
+        s_ps = {}
+        eT_ps = {}
+        o_ps = {}
+        out_ps = {}
+
+        def transpose_queries():
+            qT_ps = psum3.tile([P, NKV, P], BF16, tag="t")
+            for g in range(NKV):
+                nc.tensor.transpose(qT_ps[:, g, :], q_sb[:, g, :], ident_bf[:])
+            nc.vector.tensor_scalar(out=qT_sb[:], in0=qT_ps[:], scalar1=SCALE, scalar2=None, op0=ALU.mult)
+
+        def transpose_keys(n):
+            b, g = divmod(n, NKV)
+            kT_ps = psum3.tile([P, PACK, P], BF16, tag="t")
+            for t in range(PACK):
+                nc.tensor.transpose(kT_ps[:, t, :], k_sb[b][:, t, g * HD : (g + 1) * HD], ident_bf[:])
+            if n % 2 == 0:
+                nc.scalar.copy(out=kT_sb[n][:], in_=kT_ps[:].rearrange("d t p -> d (t p)"))
+            else:
+                nc.vector.tensor_copy(out=kT_sb[n][:], in_=kT_ps[:].rearrange("d t p -> d (t p)"))
+
+        def scores_and_maximum(n):
+            g = n % NKV
+            s_ps[n] = psum3.tile([P, M], F32, tag="s", name="s_ps")
+            nc.tensor.matmul(s_ps[n][:], lhsT=qT_sb[:, g, :], rhs=kT_sb[n][:], start=True, stop=True)
+            nc.vector.tensor_reduce(out=neg_max[:, n : n + 1], in_=s_ps[n][:], axis=AXIS.X, op=ALU.max, negate=True)
+
+        def exponentials(n):
+            nc.scalar.activation(
+                out=e_sb[n][:].rearrange("q (u p i) -> q u p i", u=2, i=2),
+                in_=s_ps[n][:].rearrange("q (u i p) -> q u p i", u=2, i=2),
+                func=ACT.Exp,
+                bias=neg_max[:, n : n + 1],
+                scale=1.0,
+                accum_out=row_sum[:, n : n + 1],
+            )
+
+        def transpose_weights(n):
+            eT_ps[n] = psum3.tile([P, 2, P], F32, tag="t", name="eT_ps")
+            e_words = e_sb[n][:].bitcast(F32)
+            for u in range(2):
+                nc.tensor.transpose(eT_ps[n][:, u, :], e_words[:, u * P : (u + 1) * P], ident_f32[:])
+
+        def group_weights(n):
+            nc.scalar.copy(
+                out=e_grouped[n][:].bitcast(F32).rearrange("p (q u) -> p q u", u=2),
+                in_=eT_ps[n][:].rearrange("p u q -> p q u"),
+            )
+
+        def quantise_weights(n):
+            nc.vector.quantize_mx(out=e_codes[:, n, :].bitcast(FP8X4), scales=e_scales[:, n, :], in_=e_grouped[n][:])
+
+        def quantise_values(b, c):
+            cols = slice(c * 2 * HD, (c + 1) * 2 * HD)
+            nc.vector.tensor_copy(
+                out=v_grouped[b][:].rearrange("p (w t) -> p w t", t=PACK)[:, cols, :].rearrange("p (x i) t -> p x t i", i=4),
+                in_=v_sb[b][:, :, cols].rearrange("p t (x i) -> p x t i", i=4),
+            )
+            nc.vector.quantize_mx(
+                out=v_codes[:, b, cols].bitcast(FP8X4),
+                scales=v_scales[:, b, cols],
+                in_=v_grouped[b][:, c * 2 * HD * PACK : (c + 1) * 2 * HD * PACK],
+            )
+
+        def weighted_values(n):
+            b, g = divmod(n, NKV)
+            c, u = divmod(g, 2)
+            if u == 0:
+                o_ps[(b, c)] = psum2.tile([P, 2, HD], F32, tag="o", name="o_ps")
+            nc.tensor.matmul_mx(
+                out=o_ps[(b, c)][:, u, :],
+                lhsT=e_codes[:, n, :].bitcast(FP8X4),
+                lhsT_scale=e_scales[:, n, :],
+                rhs=v_codes[:, b, g * HD : (g + 1) * HD].bitcast(FP8X4),
+                rhs_scale=v_scales[:, b, g * HD : (g + 1) * HD],
+                start=True,
+                stop=True,
+            )
+
+        def invert_sums(n):
+            nc.vector.reciprocal(out=inv_sum[:, n - 1 : n + 1], in_=row_sum[:, n - 1 : n + 1])
+
+        def normalise(n):
+            b, g = divmod(n, NKV)
+            c, u = divmod(g, 2)
+            nc.vector.tensor_scalar(
+                out=a_sb[b * PAIRS + c][:, u * HD : (u + 1) * HD],
+                in0=o_ps[(b, c)][:, u, :],
+                scalar1=inv_sum[:, n : n + 1],
+                scalar2=None,
+                op0=ALU.mult,
+            )
+
+        def transpose_heads(b, c):
+            aT_ps = psum3.tile([P, P], F32, tag="t")
+            nc.tensor.transpose(aT_ps[:], a_sb[b * PAIRS + c][:].bitcast(F32), ident_f32[:])
+            nc.scalar.copy(
+                out=a_grouped[c][:].bitcast(F32).rearrange("p (b e j) -> p b e j", b=B, j=G)[:, b],
+                in_=aT_ps[:].rearrange("p (j e) -> p e j", j=G),
+            )
+
+        def quantise_heads(c):
+            nc.vector.quantize_mx(out=a_codes[:, c, :].bitcast(FP8X4), scales=a_scales[:, c, :], in_=a_grouped[c][:])
+
+        def quantise_projection(c, half):
+            wT_ps = psum3.tile([P, G, 2, P], F32, tag="t")
+            wo_words = wo_sb[:].rearrange("p r c j u d -> p (r c j u d)").bitcast(F32)
+            wo_words = wo_words.rearrange("p (r c j w) -> p r c j w", r=D // P, c=PAIRS, j=G)
+            for j in range(G):
+                for k in range(2):
+                    nc.tensor.transpose(wT_ps[:, j, k, :], wo_words[:, 2 * half + k, c, j, :], ident_f32[:])
+            rows = slice(half * 2 * P, (half + 1) * 2 * P)
+            nc.scalar.copy(
+                out=w_grouped[c][:].bitcast(F32).rearrange("p (n j) -> p n j", j=G)[:, rows, :],
+                in_=wT_ps[:].rearrange("p j k n -> p (k n) j"),
+            )
+            nc.vector.quantize_mx(
+                out=w_codes[:, c, rows].bitcast(FP8X4),
+                scales=w_scales[:, c, rows],
+                in_=w_grouped[c][:, half * 2 * P * PACK : (half + 1) * 2 * P * PACK],
+            )
+
+        def project(c):
+            for half in range(2):
+                cols = slice(half * D // 2, (half + 1) * D // 2)
+                if c == 0:
+                    out_ps[half] = psum3.tile([P, D // 2], F32, tag="t", name="out_ps")
+                nc.tensor.matmul_mx(
+                    out=out_ps[half][:],
+                    lhsT=a_codes[:, c, :].bitcast(FP8X4),
+                    lhsT_scale=a_scales[:, c, :],
+                    rhs=w_codes[:, c, cols].bitcast(FP8X4),
+                    rhs_scale=w_scales[:, c, cols],
+                    start=(c == 0),
+                    stop=(c == PAIRS - 1),
+                )
+
+        def store():
+            out_rows = out.rearrange("b e n -> (b e) n")
+            nc.scalar.copy(out=out_sb[:, : D // 2], in_=out_ps[0][:])
+            nc.vector.tensor_copy(out=out_sb[:, D // 2 :], in_=out_ps[1][:])
+            for half in range(2):
+                cols = slice(half * D // 2, (half + 1) * D // 2)
+                nc.sync.dma_start(out=out_rows[:, cols], in_=out_sb[:, cols])
+
+        def unit(n):
+            return 0 <= n < UNITS
+
+        transpose_queries()
+        for n in range(KEYS_AHEAD):
+            transpose_keys(n)
+        for n in range(SCORES_AHEAD):
+            scores_and_maximum(n)
+        for r in range(UNITS + 5):
+            if unit(r - 2):
+                quantise_weights(r - 2)
+            if SCORES_AHEAD <= r + SCORES_AHEAD < UNITS:
+                scores_and_maximum(r + SCORES_AHEAD)
+            if unit(r - 1):
+                transpose_weights(r - 1)
+            if unit(r - 5) and (r - 5) % 2 == 1:
+                transpose_heads((r - 5) // NKV, ((r - 5) % NKV) // 2)
+                if r - 5 == NKV + 1:
+                    quantise_heads(0)
+            if unit(r - 3):
+                weighted_values(r - 3)
+            if unit(r - 1) and (r - 1) % 2 == 1:
+                invert_sums(r - 1)
+            if unit(r):
+                exponentials(r)
+            if unit(r - 1):
+                group_weights(r - 1)
+            if unit(r - 3):
+                normalise(r - 3)
+            if KEYS_AHEAD <= r + KEYS_AHEAD < UNITS:
+                transpose_keys(r + KEYS_AHEAD)
+            if r % 2 == 0 and r < 2 * B * PAIRS:
+                quantise_values(r // 2 // PAIRS, r // 2 % PAIRS)
+            if 0 <= r - (UNITS - 1) < 2 * PAIRS:
+                quantise_projection((r - (UNITS - 1)) // 2, (r - (UNITS - 1)) % 2)
+        project(0)
+        quantise_heads(1)
+        project(1)
+        store()

@@ -19,8 +19,8 @@ P = 128
 PACK = 4
 UNITS = B * NKV
 PAIRS = NKV // 2
-KEYS_AHEAD = 4
-SCORES_AHEAD = 2
+KEYS_AHEAD = 3
+WO_ROUND = UNITS - 1
 
 FLOPS = 2 * B * NH * E * HD * M * 2 + 2 * B * E * NH * HD * D
 
@@ -39,10 +39,14 @@ def tile_qwen2dymemdecoderlayer_pa_s_kernel(tc, q_pos, k_mem, v_mem, Wo, out):
             nc.sync.dma_start(out=q_sb[j * E : (j + 1) * E, :, :], in_=q_view[j])
         k_sb = [keep.tile([P, PACK, NKV * HD], BF16, name="k_sb%d" % b) for b in range(B)]
         v_sb = [keep.tile([P, PACK, NKV * HD], BF16, name="v_sb%d" % b) for b in range(B)]
+        k_view = [k_mem[b].rearrange("(p t) g d -> p t (g d)", t=PACK) for b in range(B)]
+        v_view = [v_mem[b].rearrange("(p t) g d -> p t (g d)", t=PACK) for b in range(B)]
+        for c in range(PAIRS):
+            cols = slice(c * 2 * HD, (c + 1) * 2 * HD)
+            nc.sync.dma_start(out=k_sb[0][:, :, cols], in_=k_view[0][:, :, cols])
+        nc.sync.dma_start(out=k_sb[1][:], in_=k_view[1])
         for b in range(B):
-            nc.sync.dma_start(out=k_sb[b][:], in_=k_mem[b].rearrange("(p t) g d -> p t (g d)", t=PACK))
-        for b in range(B):
-            nc.sync.dma_start(out=v_sb[b][:], in_=v_mem[b].rearrange("(p t) g d -> p t (g d)", t=PACK))
+            nc.sync.dma_start(out=v_sb[b][:], in_=v_view[b])
         wo_sb = keep.tile([P, D // P, PAIRS, G, 2, HD], BF16, name="wo_sb")
         wo_view = Wo.rearrange("(r p) (c u j d) -> c u j p r d", p=P, c=PAIRS, u=2, j=G)
         for c in range(PAIRS):
@@ -94,10 +98,10 @@ def tile_qwen2dymemdecoderlayer_pa_s_kernel(tc, q_pos, k_mem, v_mem, Wo, out):
             kT_ps = psum3.tile([P, PACK, P], BF16, tag="t")
             for t in range(PACK):
                 nc.tensor.transpose(kT_ps[:, t, :], k_sb[b][:, t, g * HD : (g + 1) * HD], ident_bf[:])
-            if n % 2 == 0:
-                nc.scalar.copy(out=kT_sb[n][:], in_=kT_ps[:].rearrange("d t p -> d (t p)"))
-            else:
+            if b == 0 and n % 2 == 1:
                 nc.vector.tensor_copy(out=kT_sb[n][:], in_=kT_ps[:].rearrange("d t p -> d (t p)"))
+            else:
+                nc.scalar.copy(out=kT_sb[n][:], in_=kT_ps[:].rearrange("d t p -> d (t p)"))
 
         def scores_and_maximum(n):
             g = n % NKV
@@ -182,7 +186,7 @@ def tile_qwen2dymemdecoderlayer_pa_s_kernel(tc, q_pos, k_mem, v_mem, Wo, out):
         def quantise_heads(c):
             nc.vector.quantize_mx(out=a_codes[:, c, :].bitcast(FP8X4), scales=a_scales[:, c, :], in_=a_grouped[c][:])
 
-        def quantise_projection(c, half):
+        def transpose_projection(c, half):
             wT_ps = psum3.tile([P, G, 2, P], F32, tag="t")
             wo_words = wo_sb[:].rearrange("p r c j u d -> p (r c j u d)").bitcast(F32)
             wo_words = wo_words.rearrange("p (r c j w) -> p r c j w", r=D // P, c=PAIRS, j=G)
@@ -194,6 +198,9 @@ def tile_qwen2dymemdecoderlayer_pa_s_kernel(tc, q_pos, k_mem, v_mem, Wo, out):
                 out=w_grouped[c][:].bitcast(F32).rearrange("p (n j) -> p n j", j=G)[:, rows, :],
                 in_=wT_ps[:].rearrange("p j k n -> p (k n) j"),
             )
+
+        def quantise_projection(c, half):
+            rows = slice(half * 2 * P, (half + 1) * 2 * P)
             nc.vector.quantize_mx(
                 out=w_codes[:, c, rows].bitcast(FP8X4),
                 scales=w_scales[:, c, rows],
@@ -227,38 +234,35 @@ def tile_qwen2dymemdecoderlayer_pa_s_kernel(tc, q_pos, k_mem, v_mem, Wo, out):
             return 0 <= n < UNITS
 
         transpose_queries()
-        for n in range(KEYS_AHEAD):
-            transpose_keys(n)
-        for n in range(SCORES_AHEAD):
-            scores_and_maximum(n)
-        for r in range(UNITS + 5):
-            if unit(r - 2):
-                quantise_weights(r - 2)
-            if SCORES_AHEAD <= r + SCORES_AHEAD < UNITS:
-                scores_and_maximum(r + SCORES_AHEAD)
-            if unit(r - 1):
-                transpose_weights(r - 1)
-            if unit(r - 5) and (r - 5) % 2 == 1:
-                transpose_heads((r - 5) // NKV, ((r - 5) % NKV) // 2)
-                if r - 5 == NKV + 1:
-                    quantise_heads(0)
-            if unit(r - 3):
-                weighted_values(r - 3)
+        for r in range(-KEYS_AHEAD, WO_ROUND + 2 + 2 * PAIRS):
+            if 0 <= r - WO_ROUND < 2 * PAIRS:
+                transpose_projection((r - WO_ROUND) // 2, (r - WO_ROUND) % 2)
             if unit(r - 1) and (r - 1) % 2 == 1:
                 invert_sums(r - 1)
             if unit(r):
                 exponentials(r)
-            if unit(r - 1):
-                group_weights(r - 1)
-            if unit(r - 3):
-                normalise(r - 3)
-            if KEYS_AHEAD <= r + KEYS_AHEAD < UNITS:
+            if 0 <= r - WO_ROUND - 2 < 2 * PAIRS:
+                quantise_projection((r - WO_ROUND - 2) // 2, (r - WO_ROUND - 2) % 2)
+            if unit(r + 1):
+                scores_and_maximum(r + 1)
+            if unit(r - 2):
+                quantise_weights(r - 2)
+            if unit(r + KEYS_AHEAD):
                 transpose_keys(r + KEYS_AHEAD)
-            if r % 2 == 0 and r < 2 * B * PAIRS:
+            if unit(r - 3) and (r - 3) % 2 == 1:
+                weighted_values(r - 4)
+                weighted_values(r - 3)
+                normalise(r - 4)
+                normalise(r - 3)
+            if unit(r - 1):
+                transpose_weights(r - 1)
+                group_weights(r - 1)
+            if unit(r) and r % 2 == 1:
                 quantise_values(r // 2 // PAIRS, r // 2 % PAIRS)
-            if 0 <= r - (UNITS - 1) < 2 * PAIRS:
-                quantise_projection((r - (UNITS - 1)) // 2, (r - (UNITS - 1)) % 2)
-        project(0)
-        quantise_heads(1)
-        project(1)
+        for c in range(PAIRS):
+            for b in range(B):
+                transpose_heads(b, c)
+        for c in range(PAIRS):
+            quantise_heads(c)
+            project(c)
         store()

@@ -134,12 +134,15 @@ def tile_qwen2dymemdecoderlayer_pa_s_kernel(tc, q_pos, k_mem, v_mem, Wo, out):
         def quantise_weights(n):
             nc.vector.quantize_mx(out=e_codes[:, n, :].bitcast(FP8X4), scales=e_scales[:, n, :], in_=e_grouped[n][:])
 
-        def quantise_values(b, c):
+        def regroup_values(b, c):
             cols = slice(c * 2 * HD, (c + 1) * 2 * HD)
             nc.vector.tensor_copy(
                 out=v_grouped[b][:].rearrange("p (w t) -> p w t", t=PACK)[:, cols, :].rearrange("p (x i) t -> p x t i", i=4),
                 in_=v_sb[b][:, :, cols].rearrange("p t (x i) -> p x t i", i=4),
             )
+
+        def quantise_values(b, c):
+            cols = slice(c * 2 * HD, (c + 1) * 2 * HD)
             nc.vector.quantize_mx(
                 out=v_codes[:, b, cols].bitcast(FP8X4),
                 scales=v_scales[:, b, cols],
@@ -247,6 +250,8 @@ def tile_qwen2dymemdecoderlayer_pa_s_kernel(tc, q_pos, k_mem, v_mem, Wo, out):
                 scores_and_maximum(r + 1)
             if unit(r - 2):
                 quantise_weights(r - 2)
+            if unit(r - 1) and r % 2 == 0:
+                quantise_values((r - 1) // 2 // PAIRS, (r - 1) // 2 % PAIRS)
             if unit(r + KEYS_AHEAD):
                 transpose_keys(r + KEYS_AHEAD)
             if unit(r - 3) and (r - 3) % 2 == 1:
@@ -258,7 +263,7 @@ def tile_qwen2dymemdecoderlayer_pa_s_kernel(tc, q_pos, k_mem, v_mem, Wo, out):
                 transpose_weights(r - 1)
                 group_weights(r - 1)
             if unit(r) and r % 2 == 1:
-                quantise_values(r // 2 // PAIRS, r // 2 % PAIRS)
+                regroup_values(r // 2 // PAIRS, r // 2 % PAIRS)
         for c in range(PAIRS):
             for b in range(B):
                 transpose_heads(b, c)

@@ -33,10 +33,8 @@ def tile_qwen2dymemdecoderlayer_pa_s_kernel(tc, q_pos, k_mem, v_mem, Wo, out):
         psum2 = ctx.enter_context(tc.psum_pool(name="psum2", bufs=2))
         ctx.enter_context(tc.manual_schedule())
 
-        q_sb = keep.tile([P, NKV, HD], BF16, name="q_sb")
-        q_view = q_pos.rearrange("e (g j) d -> j e g d", j=G)
-        for j in range(G):
-            nc.sync.dma_start(out=q_sb[j * E : (j + 1) * E, :, :], in_=q_view[j])
+        q_sb = keep.tile([P, NH // 2, HD], BF16, name="q_sb")
+        nc.sync.dma_start(out=q_sb[:], in_=q_pos.rearrange("e (x h) d -> (e x) h d", x=2))
         k_sb = [keep.tile([P, PACK, NKV * HD], BF16, name="k_sb%d" % b) for b in range(B)]
         v_sb = [keep.tile([P, PACK, NKV * HD], BF16, name="v_sb%d" % b) for b in range(B)]
         k_view = [k_mem[b].rearrange("(p t) g d -> p t (g d)", t=PACK) for b in range(B)]
@@ -88,10 +86,16 @@ def tile_qwen2dymemdecoderlayer_pa_s_kernel(tc, q_pos, k_mem, v_mem, Wo, out):
         out_ps = {}
 
         def transpose_queries():
-            qT_ps = psum3.tile([P, NKV, P], BF16, tag="t")
-            for g in range(NKV):
-                nc.tensor.transpose(qT_ps[:, g, :], q_sb[:, g, :], ident_bf[:])
-            nc.vector.tensor_scalar(out=qT_sb[:], in0=qT_ps[:], scalar1=SCALE, scalar2=None, op0=ALU.mult)
+            qT_ps = psum3.tile([P, NH // 2, P], BF16, tag="t")
+            for h in range(NH // 2):
+                nc.tensor.transpose(qT_ps[:, h, :], q_sb[:, h, :], ident_bf[:])
+            nc.vector.tensor_scalar(
+                out=qT_sb[:].rearrange("d (x y) (j e) -> d x (y j) e", x=2, j=G),
+                in0=qT_ps[:].rearrange("d h (e x) -> d x h e", x=2),
+                scalar1=SCALE,
+                scalar2=None,
+                op0=ALU.mult,
+            )
 
         def transpose_keys(n):
             b, g = divmod(n, NKV)

@@ -42,9 +42,9 @@ def tile_qwen2dymemdecoderlayer_pa_s_kernel(tc, q_pos, k_mem, v_mem, Wo, out):
         for c in range(PAIRS):
             cols = slice(c * 2 * HD, (c + 1) * 2 * HD)
             nc.sync.dma_start(out=k_sb[0][:, :, cols], in_=k_view[0][:, :, cols])
+        nc.sync.dma_start(out=v_sb[0][:], in_=v_view[0])
         nc.sync.dma_start(out=k_sb[1][:], in_=k_view[1])
-        for b in range(B):
-            nc.sync.dma_start(out=v_sb[b][:], in_=v_view[b])
+        nc.sync.dma_start(out=v_sb[1][:], in_=v_view[1])
         wo_sb = keep.tile([P, D // P, PAIRS, G, 2, HD], BF16, name="wo_sb")
         wo_view = Wo.rearrange("(r p) (c u j d) -> c u j p r d", p=P, c=PAIRS, u=2, j=G)
         for c in range(PAIRS):
@@ -102,7 +102,7 @@ def tile_qwen2dymemdecoderlayer_pa_s_kernel(tc, q_pos, k_mem, v_mem, Wo, out):
             kT_ps = psum3.tile([P, PACK, P], BF16, tag="t")
             for t in range(PACK):
                 nc.tensor.transpose(kT_ps[:, t, :], k_sb[b][:, t, g * HD : (g + 1) * HD], ident_bf[:])
-            if b == 0 and n % 2 == 1:
+            if n in (1, 3, 5):
                 nc.vector.tensor_copy(out=kT_sb[n][:], in_=kT_ps[:].rearrange("d t p -> d (t p)"))
             else:
                 nc.scalar.copy(out=kT_sb[n][:], in_=kT_ps[:].rearrange("d t p -> d (t p)"))
@@ -140,10 +140,20 @@ def tile_qwen2dymemdecoderlayer_pa_s_kernel(tc, q_pos, k_mem, v_mem, Wo, out):
 
         def regroup_values(b, c):
             cols = slice(c * 2 * HD, (c + 1) * 2 * HD)
-            nc.vector.tensor_copy(
-                out=v_grouped[b][:].rearrange("p (w t) -> p w t", t=PACK)[:, cols, :].rearrange("p (x i) t -> p x t i", i=4),
-                in_=v_sb[b][:, :, cols].rearrange("p t (x i) -> p x t i", i=4),
-            )
+            if b == 0:
+                nc.gpsimd.tensor_scalar(
+                    out=v_grouped[b][:].rearrange("p (w t) -> p w t", t=PACK)[:, cols, :],
+                    in0=v_sb[b][:, :, cols].rearrange("p t w -> p w t"),
+                    scalar1=1.0,
+                    scalar2=0.0,
+                    op0=ALU.mult,
+                    op1=ALU.add,
+                )
+            else:
+                nc.vector.tensor_copy(
+                    out=v_grouped[b][:].rearrange("p (w t) -> p w t", t=PACK)[:, cols, :].rearrange("p (x i) t -> p x t i", i=4),
+                    in_=v_sb[b][:, :, cols].rearrange("p t (x i) -> p x t i", i=4),
+                )
 
         def quantise_values(b, c):
             cols = slice(c * 2 * HD, (c + 1) * 2 * HD)
@@ -174,12 +184,11 @@ def tile_qwen2dymemdecoderlayer_pa_s_kernel(tc, q_pos, k_mem, v_mem, Wo, out):
         def normalise(n):
             b, g = divmod(n, NKV)
             c, u = divmod(g, 2)
-            nc.vector.tensor_scalar(
-                out=a_sb[b * PAIRS + c][:, u * HD : (u + 1) * HD],
-                in0=o_ps[(b, c)][:, u, :],
-                scalar1=inv_sum[:, n : n + 1],
-                scalar2=None,
-                op0=ALU.mult,
+            nc.vector.tensor_tensor(
+                out=a_sb[b * PAIRS + c][:].rearrange("q (u d) -> q u d", u=2),
+                in0=o_ps[(b, c)][:],
+                in1=inv_sum[:, n - 1 : n + 1].unsqueeze(2).to_broadcast([P, 2, HD]),
+                op=ALU.mult,
             )
 
         def transpose_heads(b, c):
@@ -261,7 +270,6 @@ def tile_qwen2dymemdecoderlayer_pa_s_kernel(tc, q_pos, k_mem, v_mem, Wo, out):
             if unit(r - 3) and (r - 3) % 2 == 1:
                 weighted_values(r - 4)
                 weighted_values(r - 3)
-                normalise(r - 4)
                 normalise(r - 3)
             if unit(r - 1):
                 transpose_weights(r - 1)

@@ -19,8 +19,6 @@ P = 128
 PACK = 4
 UNITS = B * NKV
 PAIRS = NKV // 2
-KEYS_AHEAD = 3
-WO_ROUND = UNITS - 1
 
 FLOPS = 2 * B * NH * E * HD * M * 2 + 2 * B * E * NH * HD * D
 
@@ -30,7 +28,8 @@ def tile_qwen2dymemdecoderlayer_pa_s_kernel(tc, q_pos, k_mem, v_mem, Wo, out):
     with ExitStack() as ctx:
         keep = ctx.enter_context(tc.tile_pool(name="keep", bufs=1))
         psum3 = ctx.enter_context(tc.psum_pool(name="psum3", bufs=3))
-        psum2 = ctx.enter_context(tc.psum_pool(name="psum2", bufs=2))
+        psum4 = ctx.enter_context(tc.psum_pool(name="psum4", bufs=4))
+        psum1 = ctx.enter_context(tc.psum_pool(name="psum1", bufs=1))
         ctx.enter_context(tc.manual_schedule())
 
         q_sb = keep.tile([P, NH // 2, HD], BF16, name="q_sb")
@@ -42,9 +41,9 @@ def tile_qwen2dymemdecoderlayer_pa_s_kernel(tc, q_pos, k_mem, v_mem, Wo, out):
         for c in range(PAIRS):
             cols = slice(c * 2 * HD, (c + 1) * 2 * HD)
             nc.sync.dma_start(out=k_sb[0][:, :, cols], in_=k_view[0][:, :, cols])
-        nc.sync.dma_start(out=v_sb[0][:], in_=v_view[0])
         nc.sync.dma_start(out=k_sb[1][:], in_=k_view[1])
-        nc.sync.dma_start(out=v_sb[1][:], in_=v_view[1])
+        for b in range(B):
+            nc.sync.dma_start(out=v_sb[b][:], in_=v_view[b])
         wo_sb = keep.tile([P, D // P, PAIRS, G, 2, HD], BF16, name="wo_sb")
         wo_view = Wo.rearrange("(r p) (c u j d) -> c u j p r d", p=P, c=PAIRS, u=2, j=G)
         for c in range(PAIRS):
@@ -63,7 +62,7 @@ def tile_qwen2dymemdecoderlayer_pa_s_kernel(tc, q_pos, k_mem, v_mem, Wo, out):
         qT_sb = keep.tile([P, NKV, P], BF16, name="qT_sb")
         kT_sb = [keep.tile([P, M], BF16, name="kT_sb%d" % n) for n in range(UNITS)]
         e_sb = [keep.tile([P, M], BF16, name="e_sb%d" % n) for n in range(UNITS)]
-        e_grouped = [keep.tile([P, P * PACK], BF16, name="e_grouped%d" % n, align_bytes=64) for n in range(UNITS)]
+        e_grouped = [keep.tile([P, 2 * P * PACK], BF16, name="e_grouped%d" % n, align_bytes=64) for n in range(UNITS // 2)]
         e_codes = keep.tile([P, UNITS, P], U32, name="e_codes", align_bytes=64)
         e_scales = keep.tile([P, UNITS, P], U8, name="e_scales", align_bytes=64)
         neg_max = keep.tile([P, UNITS], F32, name="neg_max")
@@ -86,7 +85,7 @@ def tile_qwen2dymemdecoderlayer_pa_s_kernel(tc, q_pos, k_mem, v_mem, Wo, out):
         out_ps = {}
 
         def transpose_queries():
-            qT_ps = psum3.tile([P, NH // 2, P], BF16, tag="t")
+            qT_ps = psum4.tile([P, NH // 2, P], BF16, tag="t")
             for h in range(NH // 2):
                 nc.tensor.transpose(qT_ps[:, h, :], q_sb[:, h, :], ident_bf[:])
             nc.vector.tensor_scalar(
@@ -99,10 +98,10 @@ def tile_qwen2dymemdecoderlayer_pa_s_kernel(tc, q_pos, k_mem, v_mem, Wo, out):
 
         def transpose_keys(n):
             b, g = divmod(n, NKV)
-            kT_ps = psum3.tile([P, PACK, P], BF16, tag="t")
+            kT_ps = psum4.tile([P, PACK, P], BF16, tag="t")
             for t in range(PACK):
                 nc.tensor.transpose(kT_ps[:, t, :], k_sb[b][:, t, g * HD : (g + 1) * HD], ident_bf[:])
-            if n in (1, 3, 5):
+            if n % 2 == 1:
                 nc.vector.tensor_copy(out=kT_sb[n][:], in_=kT_ps[:].rearrange("d t p -> d (t p)"))
             else:
                 nc.scalar.copy(out=kT_sb[n][:], in_=kT_ps[:].rearrange("d t p -> d (t p)"))
@@ -124,19 +123,21 @@ def tile_qwen2dymemdecoderlayer_pa_s_kernel(tc, q_pos, k_mem, v_mem, Wo, out):
             )
 
         def transpose_weights(n):
-            eT_ps[n] = psum3.tile([P, 2, P], F32, tag="t", name="eT_ps")
+            eT_ps[n] = psum4.tile([P, 2, P], F32, tag="t", name="eT_ps")
             e_words = e_sb[n][:].bitcast(F32)
             for u in range(2):
                 nc.tensor.transpose(eT_ps[n][:, u, :], e_words[:, u * P : (u + 1) * P], ident_f32[:])
 
         def group_weights(n):
             nc.scalar.copy(
-                out=e_grouped[n][:].bitcast(F32).rearrange("p (q u) -> p q u", u=2),
+                out=e_grouped[n // 2][:, n % 2 * P * PACK : (n % 2 + 1) * P * PACK].bitcast(F32).rearrange("p (q u) -> p q u", u=2),
                 in_=eT_ps[n][:].rearrange("p u q -> p q u"),
             )
 
         def quantise_weights(n):
-            nc.vector.quantize_mx(out=e_codes[:, n, :].bitcast(FP8X4), scales=e_scales[:, n, :], in_=e_grouped[n][:])
+            codes = e_codes[:, n - 1 : n + 1, :].rearrange("p n q -> p (n q)")
+            scales = e_scales[:, n - 1 : n + 1, :].rearrange("p n q -> p (n q)")
+            nc.vector.quantize_mx(out=codes.bitcast(FP8X4), scales=scales, in_=e_grouped[n // 2][:])
 
         def regroup_values(b, c):
             cols = slice(c * 2 * HD, (c + 1) * 2 * HD)
@@ -167,7 +168,7 @@ def tile_qwen2dymemdecoderlayer_pa_s_kernel(tc, q_pos, k_mem, v_mem, Wo, out):
             b, g = divmod(n, NKV)
             c, u = divmod(g, 2)
             if u == 0:
-                o_ps[(b, c)] = psum2.tile([P, 2, HD], F32, tag="o", name="o_ps")
+                o_ps[(b, c)] = psum1.tile([P, 2, HD], F32, tag="o", name="o_ps")
             nc.tensor.matmul_mx(
                 out=o_ps[(b, c)][:, u, :],
                 lhsT=e_codes[:, n, :].bitcast(FP8X4),
@@ -192,7 +193,7 @@ def tile_qwen2dymemdecoderlayer_pa_s_kernel(tc, q_pos, k_mem, v_mem, Wo, out):
             )
 
         def transpose_heads(b, c):
-            aT_ps = psum3.tile([P, P], F32, tag="t")
+            aT_ps = psum4.tile([P, P], F32, tag="t")
             nc.tensor.transpose(aT_ps[:], a_sb[b * PAIRS + c][:].bitcast(F32), ident_f32[:])
             nc.scalar.copy(
                 out=a_grouped[c][:].bitcast(F32).rearrange("p (b e j) -> p b e j", b=B, j=G)[:, b],
@@ -203,7 +204,7 @@ def tile_qwen2dymemdecoderlayer_pa_s_kernel(tc, q_pos, k_mem, v_mem, Wo, out):
             nc.vector.quantize_mx(out=a_codes[:, c, :].bitcast(FP8X4), scales=a_scales[:, c, :], in_=a_grouped[c][:])
 
         def transpose_projection(c, half):
-            wT_ps = psum3.tile([P, G, 2, P], F32, tag="t")
+            wT_ps = psum4.tile([P, G, 2, P], F32, tag="t")
             wo_words = wo_sb[:].rearrange("p r c j u d -> p (r c j u d)").bitcast(F32)
             wo_words = wo_words.rearrange("p (r c j w) -> p r c j w", r=D // P, c=PAIRS, j=G)
             for j in range(G):
@@ -223,63 +224,101 @@ def tile_qwen2dymemdecoderlayer_pa_s_kernel(tc, q_pos, k_mem, v_mem, Wo, out):
                 in_=w_grouped[c][:, half * 2 * P * PACK : (half + 1) * 2 * P * PACK],
             )
 
-        def project(c):
-            for half in range(2):
-                cols = slice(half * D // 2, (half + 1) * D // 2)
-                if c == 0:
-                    out_ps[half] = psum3.tile([P, D // 2], F32, tag="t", name="out_ps")
-                nc.tensor.matmul_mx(
-                    out=out_ps[half][:],
-                    lhsT=a_codes[:, c, :].bitcast(FP8X4),
-                    lhsT_scale=a_scales[:, c, :],
-                    rhs=w_codes[:, c, cols].bitcast(FP8X4),
-                    rhs_scale=w_scales[:, c, cols],
-                    start=(c == 0),
-                    stop=(c == PAIRS - 1),
-                )
+        def project(c, half):
+            cols = slice(half * D // 2, (half + 1) * D // 2)
+            if c == 0:
+                out_ps[half] = psum3.tile([P, D // 2], F32, tag="s", name="out_ps")
+            nc.tensor.matmul_mx(
+                out=out_ps[half][:],
+                lhsT=a_codes[:, c, :].bitcast(FP8X4),
+                lhsT_scale=a_scales[:, c, :],
+                rhs=w_codes[:, c, cols].bitcast(FP8X4),
+                rhs_scale=w_scales[:, c, cols],
+                start=(c == 0),
+                stop=(c == PAIRS - 1),
+            )
 
-        def store():
+        def store(half):
             out_rows = out.rearrange("b e n -> (b e) n")
-            nc.scalar.copy(out=out_sb[:, : D // 2], in_=out_ps[0][:])
-            nc.vector.tensor_copy(out=out_sb[:, D // 2 :], in_=out_ps[1][:])
-            for half in range(2):
-                cols = slice(half * D // 2, (half + 1) * D // 2)
-                nc.sync.dma_start(out=out_rows[:, cols], in_=out_sb[:, cols])
+            cols = slice(half * D // 2, (half + 1) * D // 2)
+            if half == 0:
+                nc.scalar.copy(out=out_sb[:, cols], in_=out_ps[half][:])
+            else:
+                nc.vector.tensor_copy(out=out_sb[:, cols], in_=out_ps[half][:])
+            nc.sync.dma_start(out=out_rows[:, cols], in_=out_sb[:, cols])
 
         def unit(n):
             return 0 <= n < UNITS
 
         transpose_queries()
-        for r in range(-KEYS_AHEAD, WO_ROUND + 2 + 2 * PAIRS):
-            if 0 <= r - WO_ROUND < 2 * PAIRS:
-                transpose_projection((r - WO_ROUND) // 2, (r - WO_ROUND) % 2)
-            if unit(r - 1) and (r - 1) % 2 == 1:
-                invert_sums(r - 1)
-            if unit(r):
-                exponentials(r)
-            if 0 <= r - WO_ROUND - 2 < 2 * PAIRS:
-                quantise_projection((r - WO_ROUND - 2) // 2, (r - WO_ROUND - 2) % 2)
-            if unit(r + 1):
-                scores_and_maximum(r + 1)
-            if unit(r - 2):
-                quantise_weights(r - 2)
-            if unit(r - 1) and r % 2 == 0:
-                quantise_values((r - 1) // 2 // PAIRS, (r - 1) // 2 % PAIRS)
-            if unit(r + KEYS_AHEAD):
-                transpose_keys(r + KEYS_AHEAD)
-            if unit(r - 3) and (r - 3) % 2 == 1:
-                weighted_values(r - 4)
-                weighted_values(r - 3)
-                normalise(r - 3)
+        transpose_keys(0)
+        transpose_keys(1)
+        scores_and_maximum(0)
+        transpose_keys(2)
+        scores_and_maximum(1)
+        transpose_keys(3)
+        regroup_values(0, 0)
+        regroup_values(0, 1)
+        for r in range(UNITS - 1):
+            exponentials(r)
             if unit(r - 1):
                 transpose_weights(r - 1)
+            if unit(r + 2):
+                scores_and_maximum(r + 2)
+            if unit(r - 1):
                 group_weights(r - 1)
-            if unit(r) and r % 2 == 1:
-                regroup_values(r // 2 // PAIRS, r // 2 % PAIRS)
-        for c in range(PAIRS):
-            for b in range(B):
-                transpose_heads(b, c)
-        for c in range(PAIRS):
-            quantise_heads(c)
-            project(c)
-        store()
+            if unit(r + 4):
+                transpose_keys(r + 4)
+            if r >= 5 and r % 2 == 1:
+                weighted_values(r - 5)
+                weighted_values(r - 4)
+            if r >= 3 and r % 2 == 1:
+                quantise_weights(r - 2)
+                quantise_values((r - 2) // 2 // PAIRS, (r - 2) // 2 % PAIRS)
+                invert_sums(r - 2)
+            if r >= 5 and r % 2 == 1:
+                normalise(r - 4)
+            if r == 4:
+                regroup_values(1, 0)
+            if r == 6:
+                regroup_values(1, 1)
+        exponentials(7)
+        transpose_weights(6)
+        transpose_projection(0, 0)
+        group_weights(6)
+        transpose_weights(7)
+        weighted_values(2)
+        weighted_values(3)
+        quantise_weights(5)
+        quantise_values(1, 0)
+        invert_sums(5)
+        normalise(3)
+        group_weights(7)
+        transpose_projection(0, 1)
+        quantise_values(1, 1)
+        invert_sums(7)
+        transpose_heads(0, 0)
+        weighted_values(4)
+        weighted_values(5)
+        quantise_weights(7)
+        transpose_projection(1, 0)
+        normalise(5)
+        transpose_heads(0, 1)
+        quantise_projection(0, 0)
+        weighted_values(6)
+        weighted_values(7)
+        transpose_heads(1, 0)
+        normalise(7)
+        quantise_projection(0, 1)
+        transpose_projection(1, 1)
+        transpose_heads(1, 1)
+        quantise_heads(0)
+        quantise_projection(1, 0)
+        project(0, 0)
+        project(0, 1)
+        quantise_heads(1)
+        project(1, 0)
+        quantise_projection(1, 1)
+        project(1, 1)
+        store(0)
+        store(1)

@@ -101,7 +101,7 @@ def tile_qwen2dymemdecoderlayer_pa_s_kernel(tc, q_pos, k_mem, v_mem, Wo, out):
             kT_ps = psum4.tile([P, PACK, P], BF16, tag="t")
             for t in range(PACK):
                 nc.tensor.transpose(kT_ps[:, t, :], k_sb[b][:, t, g * HD : (g + 1) * HD], ident_bf[:])
-            if n % 2 == 1:
+            if n % 2 == 1 or n == 6:
                 nc.vector.tensor_copy(out=kT_sb[n][:], in_=kT_ps[:].rearrange("d t p -> d (t p)"))
             else:
                 nc.scalar.copy(out=kT_sb[n][:], in_=kT_ps[:].rearrange("d t p -> d (t p)"))
@@ -141,7 +141,7 @@ def tile_qwen2dymemdecoderlayer_pa_s_kernel(tc, q_pos, k_mem, v_mem, Wo, out):
 
         def regroup_values(b, c):
             cols = slice(c * 2 * HD, (c + 1) * 2 * HD)
-            if b == 0:
+            if (b, c) != (1, 1):
                 nc.gpsimd.tensor_scalar(
                     out=v_grouped[b][:].rearrange("p (w t) -> p w t", t=PACK)[:, cols, :],
                     in0=v_sb[b][:, :, cols].rearrange("p t w -> p w t"),
@@ -168,7 +168,10 @@ def tile_qwen2dymemdecoderlayer_pa_s_kernel(tc, q_pos, k_mem, v_mem, Wo, out):
             b, g = divmod(n, NKV)
             c, u = divmod(g, 2)
             if u == 0:
-                o_ps[(b, c)] = psum1.tile([P, 2, HD], F32, tag="o", name="o_ps")
+                if b == 0:
+                    o_ps[(b, c)] = psum1.tile([P, 2, HD], F32, tag="o", name="o_ps")
+                else:
+                    o_ps[(b, c)] = psum3.tile([P, 2, HD], F32, tag="s", name="o_ps")
             nc.tensor.matmul_mx(
                 out=o_ps[(b, c)][:, u, :],
                 lhsT=e_codes[:, n, :].bitcast(FP8X4),
@@ -251,74 +254,76 @@ def tile_qwen2dymemdecoderlayer_pa_s_kernel(tc, q_pos, k_mem, v_mem, Wo, out):
             return 0 <= n < UNITS
 
         transpose_queries()
-        transpose_keys(0)
-        transpose_keys(1)
+        for n in range(4):
+            transpose_keys(n)
         scores_and_maximum(0)
-        transpose_keys(2)
         scores_and_maximum(1)
-        transpose_keys(3)
-        regroup_values(0, 0)
-        regroup_values(0, 1)
-        for r in range(UNITS - 1):
+        transpose_keys(4)
+        for b, c in ((0, 0), (0, 1), (1, 0)):
+            regroup_values(b, c)
+        for r in range(UNITS):
             exponentials(r)
-            if unit(r - 1):
+            if r == 0:
+                scores_and_maximum(2)
+                transpose_keys(5)
+                transpose_keys(6)
+            if r == 1:
+                scores_and_maximum(3)
+                transpose_weights(0)
+                transpose_keys(7)
+            if r >= 2:
+                if r + 2 < UNITS:
+                    scores_and_maximum(r + 2)
                 transpose_weights(r - 1)
-            if unit(r + 2):
-                scores_and_maximum(r + 2)
-            if unit(r - 1):
-                group_weights(r - 1)
-            if unit(r + 4):
-                transpose_keys(r + 4)
-            if r >= 5 and r % 2 == 1:
-                weighted_values(r - 5)
-                weighted_values(r - 4)
-            if r >= 3 and r % 2 == 1:
-                quantise_weights(r - 2)
-                quantise_values((r - 2) // 2 // PAIRS, (r - 2) // 2 % PAIRS)
-                invert_sums(r - 2)
-            if r >= 5 and r % 2 == 1:
-                normalise(r - 4)
+                group_weights(r - 2)
             if r == 4:
-                regroup_values(1, 0)
+                quantise_values(0, 0)
+                quantise_weights(1)
+                invert_sums(1)
+            if r == 5:
+                quantise_values(0, 1)
             if r == 6:
-                regroup_values(1, 1)
-        exponentials(7)
-        transpose_weights(6)
+                weighted_values(0)
+                weighted_values(1)
+                quantise_weights(3)
+                invert_sums(3)
+                normalise(1)
+                quantise_values(1, 0)
         transpose_projection(0, 0)
-        group_weights(6)
         transpose_weights(7)
         weighted_values(2)
         weighted_values(3)
+        regroup_values(1, 1)
         quantise_weights(5)
-        quantise_values(1, 0)
         invert_sums(5)
         normalise(3)
+        group_weights(6)
         group_weights(7)
         transpose_projection(0, 1)
-        quantise_values(1, 1)
-        invert_sums(7)
-        transpose_heads(0, 0)
+        transpose_projection(1, 0)
         weighted_values(4)
         weighted_values(5)
+        quantise_values(1, 1)
         quantise_weights(7)
-        transpose_projection(1, 0)
+        invert_sums(7)
         normalise(5)
-        transpose_heads(0, 1)
-        quantise_projection(0, 0)
+        transpose_projection(1, 1)
         weighted_values(6)
         weighted_values(7)
-        transpose_heads(1, 0)
+        transpose_heads(0, 0)
+        transpose_heads(0, 1)
+        quantise_projection(0, 0)
         normalise(7)
+        transpose_heads(1, 0)
         quantise_projection(0, 1)
-        transpose_projection(1, 1)
-        transpose_heads(1, 1)
-        quantise_heads(0)
         quantise_projection(1, 0)
+        quantise_heads(0)
+        transpose_heads(1, 1)
+        quantise_projection(1, 1)
         project(0, 0)
         project(0, 1)
         quantise_heads(1)
         project(1, 0)
-        quantise_projection(1, 1)
         project(1, 1)
         store(0)
         store(1)

@@ -141,7 +141,7 @@ def tile_qwen2dymemdecoderlayer_pa_s_kernel(tc, q_pos, k_mem, v_mem, Wo, out):
 
         def regroup_values(b, c):
             cols = slice(c * 2 * HD, (c + 1) * 2 * HD)
-            if (b, c) != (1, 1):
+            if b == 0:
                 nc.gpsimd.tensor_scalar(
                     out=v_grouped[b][:].rearrange("p (w t) -> p w t", t=PACK)[:, cols, :],
                     in0=v_sb[b][:, :, cols].rearrange("p t w -> p w t"),
@@ -259,8 +259,8 @@ def tile_qwen2dymemdecoderlayer_pa_s_kernel(tc, q_pos, k_mem, v_mem, Wo, out):
         scores_and_maximum(0)
         scores_and_maximum(1)
         transpose_keys(4)
-        for b, c in ((0, 0), (0, 1), (1, 0)):
-            regroup_values(b, c)
+        for c in range(PAIRS):
+            regroup_values(0, c)
         for r in range(UNITS):
             exponentials(r)
             if r == 0:
@@ -276,6 +276,8 @@ def tile_qwen2dymemdecoderlayer_pa_s_kernel(tc, q_pos, k_mem, v_mem, Wo, out):
                     scores_and_maximum(r + 2)
                 transpose_weights(r - 1)
                 group_weights(r - 2)
+            if r == 3:
+                regroup_values(1, 0)
             if r == 4:
                 quantise_values(0, 0)
                 quantise_weights(1)

@@ -58,6 +58,35 @@ def tile_qwen2dymemdecoderlayer_pa_s_kernel(tc, q_pos, k_mem, v_mem, Wo, out):
         warm = keep.tile([P, 1], F32, name="warm")
         nc.vector.memset(warm[:], 0.0)
         nc.scalar.activation(out=warm[:], in_=warm[:], func=ACT.Exp)
+        idle_in = keep.tile([P, P * PACK], BF16, name="idle_in", align_bytes=64)
+        idle_codes = keep.tile([P, P], U32, name="idle_codes", align_bytes=64)
+        idle_scales = keep.tile([P, P], U8, name="idle_scales", align_bytes=64)
+        nc.vector.memset(idle_in[:].bitcast(F32), 0.0)
+        nc.vector.quantize_mx(out=idle_codes[:].bitcast(FP8X4), scales=idle_scales[:], in_=idle_in[:])
+
+        def stream_zeros(bank, count):
+            for i in range(count):
+                nc.tensor.matmul_mx(
+                    out=bank[:, :P],
+                    lhsT=idle_codes[:].bitcast(FP8X4),
+                    lhsT_scale=idle_scales[:],
+                    rhs=idle_codes[:].bitcast(FP8X4),
+                    rhs_scale=idle_scales[:],
+                    start=True,
+                    stop=True,
+                )
+
+        def stream_values(bank, count):
+            for i in range(count):
+                nc.tensor.matmul_mx(
+                    out=bank,
+                    lhsT=e_codes[:, 0, :].bitcast(FP8X4),
+                    lhsT_scale=e_scales[:, 0, :],
+                    rhs=v_codes[:, 0, :].bitcast(FP8X4),
+                    rhs_scale=v_scales[:, 0, :],
+                    start=True,
+                    stop=True,
+                )
 
         qT_sb = keep.tile([P, NKV, P], BF16, name="qT_sb")
         kT_sb = [keep.tile([P, M], BF16, name="kT_sb%d" % n) for n in range(UNITS)]
@@ -170,6 +199,8 @@ def tile_qwen2dymemdecoderlayer_pa_s_kernel(tc, q_pos, k_mem, v_mem, Wo, out):
             if u == 0:
                 if b == 0:
                     o_ps[(b, c)] = psum1.tile([P, 2, HD], F32, tag="o", name="o_ps")
+                    if c == 0:
+                        stream_zeros(o_ps[(b, c)][:, 0, :], 6)
                 else:
                     o_ps[(b, c)] = psum3.tile([P, 2, HD], F32, tag="s", name="o_ps")
             nc.tensor.matmul_mx(
@@ -229,10 +260,10 @@ def tile_qwen2dymemdecoderlayer_pa_s_kernel(tc, q_pos, k_mem, v_mem, Wo, out):
 
         def project(c, half):
             cols = slice(half * D // 2, (half + 1) * D // 2)
-            if c == 0:
-                out_ps[half] = psum3.tile([P, D // 2], F32, tag="s", name="out_ps")
+            if half not in out_ps:
+                out_ps[half] = psum3.tile([P, D], F32, tag="s", name="out_ps")
             nc.tensor.matmul_mx(
-                out=out_ps[half][:],
+                out=out_ps[half][:, : D // 2],
                 lhsT=a_codes[:, c, :].bitcast(FP8X4),
                 lhsT_scale=a_scales[:, c, :],
                 rhs=w_codes[:, c, cols].bitcast(FP8X4),
@@ -245,16 +276,21 @@ def tile_qwen2dymemdecoderlayer_pa_s_kernel(tc, q_pos, k_mem, v_mem, Wo, out):
             out_rows = out.rearrange("b e n -> (b e) n")
             cols = slice(half * D // 2, (half + 1) * D // 2)
             if half == 0:
-                nc.scalar.copy(out=out_sb[:, cols], in_=out_ps[half][:])
+                nc.scalar.copy(out=out_sb[:, cols], in_=out_ps[half][:, : D // 2])
             else:
-                nc.vector.tensor_copy(out=out_sb[:, cols], in_=out_ps[half][:])
+                nc.vector.tensor_copy(out=out_sb[:, cols], in_=out_ps[half][:, : D // 2])
             nc.sync.dma_start(out=out_rows[:, cols], in_=out_sb[:, cols])
 
         def unit(n):
             return 0 <= n < UNITS
 
+        head_ps = psum1.tile([P, P], F32, tag="o", name="head_ps")
+        stream_zeros(head_ps, 10)
         transpose_queries()
+        stream_zeros(head_ps, 6)
         for n in range(4):
+            if n == 2:
+                stream_zeros(head_ps, 8)
             transpose_keys(n)
         scores_and_maximum(0)
         scores_and_maximum(1)
@@ -291,8 +327,11 @@ def tile_qwen2dymemdecoderlayer_pa_s_kernel(tc, q_pos, k_mem, v_mem, Wo, out):
                 invert_sums(3)
                 normalise(1)
                 quantise_values(1, 0)
+        out_ps[0] = psum3.tile([P, D], F32, tag="s", name="out_ps")
         transpose_projection(0, 0)
+        stream_values(out_ps[0][:], 1)
         transpose_weights(7)
+        stream_values(out_ps[0][:], 1)
         weighted_values(2)
         weighted_values(3)
         regroup_values(1, 1)
@@ -310,6 +349,7 @@ def tile_qwen2dymemdecoderlayer_pa_s_kernel(tc, q_pos, k_mem, v_mem, Wo, out):
         invert_sums(7)
         normalise(5)
         transpose_projection(1, 1)
+        stream_values(out_ps[0][:], 1)
         weighted_values(6)
         weighted_values(7)
         transpose_heads(0, 0)
@@ -322,6 +362,7 @@ def tile_qwen2dymemdecoderlayer_pa_s_kernel(tc, q_pos, k_mem, v_mem, Wo, out):
         quantise_heads(0)
         transpose_heads(1, 1)
         quantise_projection(1, 1)
+        stream_values(out_ps[0][:], 2)
         project(0, 0)
         project(0, 1)
         quantise_heads(1)

@@ -112,11 +112,12 @@ def tile_qwen2dymemdecoderlayer_pa_s_kernel(tc, q_pos, k_mem, v_mem, Wo, out):
         eT_ps = {}
         o_ps = {}
         out_ps = {}
+        wT_ps = {}
 
         def transpose_queries():
             qT_ps = psum4.tile([P, NH // 2, P], BF16, tag="t")
             for h in range(NH // 2):
-                nc.tensor.transpose(qT_ps[:, h, :], q_sb[:, h, :], ident_bf[:])
+                nc.tensor.matmul(qT_ps[:, h, :], lhsT=q_sb[:, h, :], rhs=ident_bf[:], start=True, stop=True)
             nc.vector.tensor_scalar(
                 out=qT_sb[:].rearrange("d (x y) (j e) -> d x (y j) e", x=2, j=G),
                 in0=qT_ps[:].rearrange("d h (e x) -> d x h e", x=2),
@@ -200,7 +201,7 @@ def tile_qwen2dymemdecoderlayer_pa_s_kernel(tc, q_pos, k_mem, v_mem, Wo, out):
                 if b == 0:
                     o_ps[(b, c)] = psum1.tile([P, 2, HD], F32, tag="o", name="o_ps")
                     if c == 0:
-                        stream_zeros(o_ps[(b, c)][:, 0, :], 6)
+                        stream_zeros(o_ps[(b, c)][:, 0, :], 8)
                 else:
                     o_ps[(b, c)] = psum3.tile([P, 2, HD], F32, tag="s", name="o_ps")
             nc.tensor.matmul_mx(
@@ -238,16 +239,18 @@ def tile_qwen2dymemdecoderlayer_pa_s_kernel(tc, q_pos, k_mem, v_mem, Wo, out):
             nc.vector.quantize_mx(out=a_codes[:, c, :].bitcast(FP8X4), scales=a_scales[:, c, :], in_=a_grouped[c][:])
 
         def transpose_projection(c, half):
-            wT_ps = psum4.tile([P, G, 2, P], F32, tag="t")
+            wT_ps[(c, half)] = psum4.tile([P, G, 2, P], F32, tag="t", name="wT_ps")
             wo_words = wo_sb[:].rearrange("p r c j u d -> p (r c j u d)").bitcast(F32)
             wo_words = wo_words.rearrange("p (r c j w) -> p r c j w", r=D // P, c=PAIRS, j=G)
             for j in range(G):
                 for k in range(2):
-                    nc.tensor.transpose(wT_ps[:, j, k, :], wo_words[:, 2 * half + k, c, j, :], ident_f32[:])
+                    nc.tensor.transpose(wT_ps[(c, half)][:, j, k, :], wo_words[:, 2 * half + k, c, j, :], ident_f32[:])
+
+        def group_projection(c, half):
             rows = slice(half * 2 * P, (half + 1) * 2 * P)
             nc.scalar.copy(
                 out=w_grouped[c][:].bitcast(F32).rearrange("p (n j) -> p n j", j=G)[:, rows, :],
-                in_=wT_ps[:].rearrange("p j k n -> p (k n) j"),
+                in_=wT_ps[(c, half)][:].rearrange("p j k n -> p (k n) j"),
             )
 
         def quantise_projection(c, half):
@@ -285,15 +288,15 @@ def tile_qwen2dymemdecoderlayer_pa_s_kernel(tc, q_pos, k_mem, v_mem, Wo, out):
             return 0 <= n < UNITS
 
         head_ps = psum1.tile([P, P], F32, tag="o", name="head_ps")
-        stream_zeros(head_ps, 10)
+        stream_zeros(head_ps, 11)
         transpose_queries()
+        transpose_keys(0)
+        transpose_keys(1)
         stream_zeros(head_ps, 6)
-        for n in range(4):
-            if n == 2:
-                stream_zeros(head_ps, 8)
-            transpose_keys(n)
         scores_and_maximum(0)
+        transpose_keys(2)
         scores_and_maximum(1)
+        transpose_keys(3)
         transpose_keys(4)
         for c in range(PAIRS):
             regroup_values(0, c)
@@ -304,11 +307,13 @@ def tile_qwen2dymemdecoderlayer_pa_s_kernel(tc, q_pos, k_mem, v_mem, Wo, out):
                 transpose_keys(5)
                 transpose_keys(6)
             if r == 1:
+                stream_zeros(head_ps, 5)
                 scores_and_maximum(3)
                 transpose_weights(0)
                 transpose_keys(7)
             if r >= 2:
                 if r + 2 < UNITS:
+                    stream_zeros(head_ps, (0, 0, 0, 0, 0, 1)[r])
                     scores_and_maximum(r + 2)
                 transpose_weights(r - 1)
                 group_weights(r - 2)
@@ -329,6 +334,7 @@ def tile_qwen2dymemdecoderlayer_pa_s_kernel(tc, q_pos, k_mem, v_mem, Wo, out):
                 quantise_values(1, 0)
         out_ps[0] = psum3.tile([P, D], F32, tag="s", name="out_ps")
         transpose_projection(0, 0)
+        group_projection(0, 0)
         stream_values(out_ps[0][:], 1)
         transpose_weights(7)
         stream_values(out_ps[0][:], 1)
@@ -341,7 +347,9 @@ def tile_qwen2dymemdecoderlayer_pa_s_kernel(tc, q_pos, k_mem, v_mem, Wo, out):
         group_weights(6)
         group_weights(7)
         transpose_projection(0, 1)
+        group_projection(0, 1)
         transpose_projection(1, 0)
+        group_projection(1, 0)
         weighted_values(4)
         weighted_values(5)
         quantise_values(1, 1)
@@ -349,6 +357,7 @@ def tile_qwen2dymemdecoderlayer_pa_s_kernel(tc, q_pos, k_mem, v_mem, Wo, out):
         invert_sums(7)
         normalise(5)
         transpose_projection(1, 1)
+        group_projection(1, 1)
         stream_values(out_ps[0][:], 1)
         weighted_values(6)
         weighted_values(7)

from contextlib import ExitStack

import concourse.masks as masks
import concourse.mybir as mybir

F32 = mybir.dt.float32
BF16 = mybir.dt.bfloat16
U32 = mybir.dt.uint32
U8 = mybir.dt.uint8
FP8X4 = mybir.dt.float8_e4m3fn_x4
ACT = mybir.ActivationFunctionType
ALU = mybir.AluOpType
AXIS = mybir.AxisListType

B, E, M, NH, NKV, HD, D = 2, 64, 512, 8, 4, 128, 512
G = NH // NKV
SCALE = 0.5
P = 128
PACK = 4
UNITS = B * NKV
PAIRS = NKV // 2

FLOPS = 2 * B * NH * E * HD * M * 2 + 2 * B * E * NH * HD * D


def tile_qwen2dymemdecoderlayer_pa_s_kernel(tc, q_pos, k_mem, v_mem, Wo, out):
    nc = tc.nc
    with ExitStack() as ctx:
        keep = ctx.enter_context(tc.tile_pool(name="keep", bufs=1))
        psum3 = ctx.enter_context(tc.psum_pool(name="psum3", bufs=3))
        psum4 = ctx.enter_context(tc.psum_pool(name="psum4", bufs=4))
        psum1 = ctx.enter_context(tc.psum_pool(name="psum1", bufs=1))
        ctx.enter_context(tc.manual_schedule())

        q_sb = keep.tile([P, NH // 2, HD], BF16, name="q_sb")
        nc.sync.dma_start(out=q_sb[:], in_=q_pos.rearrange("e (x h) d -> (e x) h d", x=2))
        k_sb = [keep.tile([P, PACK, NKV * HD], BF16, name="k_sb%d" % b) for b in range(B)]
        v_sb = [keep.tile([P, PACK, NKV * HD], BF16, name="v_sb%d" % b) for b in range(B)]
        k_view = [k_mem[b].rearrange("(p t) g d -> p t (g d)", t=PACK) for b in range(B)]
        v_view = [v_mem[b].rearrange("(p t) g d -> p t (g d)", t=PACK) for b in range(B)]
        for c in range(PAIRS):
            cols = slice(c * 2 * HD, (c + 1) * 2 * HD)
            nc.sync.dma_start(out=k_sb[0][:, :, cols], in_=k_view[0][:, :, cols])
        nc.sync.dma_start(out=k_sb[1][:], in_=k_view[1])
        for b in range(B):
            nc.sync.dma_start(out=v_sb[b][:], in_=v_view[b])
        wo_sb = keep.tile([P, D // P, PAIRS, G, 2, HD], BF16, name="wo_sb")
        wo_view = Wo.rearrange("(r p) (c u j d) -> c u j p r d", p=P, c=PAIRS, u=2, j=G)
        for c in range(PAIRS):
            for j in range(G):
                for u in range(2):
                    nc.sync.dma_start(out=wo_sb[:, :, c, j, u, :], in_=wo_view[c, u, j])

        ident_bf = keep.tile([P, P], BF16, name="ident_bf")
        masks.make_identity(nc, ident_bf[:])
        ident_f32 = keep.tile([P, P], F32, name="ident_f32")
        masks.make_identity(nc, ident_f32[:])
        warm = keep.tile([P, 1], F32, name="warm")
        nc.vector.memset(warm[:], 0.0)
        nc.scalar.activation(out=warm[:], in_=warm[:], func=ACT.Exp)
        idle_in = keep.tile([P, P * PACK], BF16, name="idle_in", align_bytes=64)
        idle_codes = keep.tile([P, P], U32, name="idle_codes", align_bytes=64)
        idle_scales = keep.tile([P, P], U8, name="idle_scales", align_bytes=64)
        nc.vector.memset(idle_in[:].bitcast(F32), 0.0)
        nc.vector.quantize_mx(out=idle_codes[:].bitcast(FP8X4), scales=idle_scales[:], in_=idle_in[:])

        def stream_zeros(bank, count):
            for i in range(count):
                nc.tensor.matmul_mx(
                    out=bank[:, :P],
                    lhsT=idle_codes[:].bitcast(FP8X4),
                    lhsT_scale=idle_scales[:],
                    rhs=idle_codes[:].bitcast(FP8X4),
                    rhs_scale=idle_scales[:],
                    start=True,
                    stop=True,
                )

        def stream_values(bank, count):
            for i in range(count):
                nc.tensor.matmul_mx(
                    out=bank,
                    lhsT=e_codes[:, 0, :].bitcast(FP8X4),
                    lhsT_scale=e_scales[:, 0, :],
                    rhs=v_codes[:, 0, :].bitcast(FP8X4),
                    rhs_scale=v_scales[:, 0, :],
                    start=True,
                    stop=True,
                )

        qT_sb = keep.tile([P, NKV, P], BF16, name="qT_sb")
        kT_sb = [keep.tile([P, M], BF16, name="kT_sb%d" % n) for n in range(UNITS)]
        e_sb = [keep.tile([P, M], BF16, name="e_sb%d" % n) for n in range(UNITS)]
        e_grouped = [keep.tile([P, 2 * P * PACK], BF16, name="e_grouped%d" % n, align_bytes=64) for n in range(UNITS // 2)]
        e_codes = keep.tile([P, UNITS, P], U32, name="e_codes", align_bytes=64)
        e_scales = keep.tile([P, UNITS, P], U8, name="e_scales", align_bytes=64)
        neg_max = keep.tile([P, UNITS], F32, name="neg_max")
        row_sum = keep.tile([P, UNITS], F32, name="row_sum")
        inv_sum = keep.tile([P, UNITS], F32, name="inv_sum")
        v_grouped = [keep.tile([P, NKV * HD * PACK], BF16, name="v_grouped%d" % b, align_bytes=64) for b in range(B)]
        v_codes = keep.tile([P, B, NKV * HD], U32, name="v_codes", align_bytes=64)
        v_scales = keep.tile([P, B, NKV * HD], U8, name="v_scales", align_bytes=64)
        a_sb = [keep.tile([P, 2 * HD], BF16, name="a_sb%d" % i) for i in range(B * PAIRS)]
        a_grouped = [keep.tile([P, B * E * PACK], BF16, name="a_grouped%d" % c, align_bytes=64) for c in range(PAIRS)]
        a_codes = keep.tile([P, PAIRS, B * E], U32, name="a_codes", align_bytes=64)
        a_scales = keep.tile([P, PAIRS, B * E], U8, name="a_scales", align_bytes=64)
        w_grouped = [keep.tile([P, D * PACK], BF16, name="w_grouped%d" % c, align_bytes=64) for c in range(PAIRS)]
        w_codes = keep.tile([P, PAIRS, D], U32, name="w_codes", align_bytes=64)
        w_scales = keep.tile([P, PAIRS, D], U8, name="w_scales", align_bytes=64)
        out_sb = keep.tile([P, D], F32, name="out_sb")
        s_ps = {}
        eT_ps = {}
        o_ps = {}
        out_ps = {}
        wT_ps = {}

        def transpose_queries():
            qT_ps = psum4.tile([P, NH // 2, P], BF16, tag="t")
            for h in range(NH // 2):
                nc.tensor.matmul(qT_ps[:, h, :], lhsT=q_sb[:, h, :], rhs=ident_bf[:], start=True, stop=True)
            nc.vector.tensor_scalar(
                out=qT_sb[:].rearrange("d (x y) (j e) -> d x (y j) e", x=2, j=G),
                in0=qT_ps[:].rearrange("d h (e x) -> d x h e", x=2),
                scalar1=SCALE,
                scalar2=None,
                op0=ALU.mult,
            )

        def transpose_keys(n):
            b, g = divmod(n, NKV)
            kT_ps = psum4.tile([P, PACK, P], BF16, tag="t")
            for t in range(PACK):
                nc.tensor.transpose(kT_ps[:, t, :], k_sb[b][:, t, g * HD : (g + 1) * HD], ident_bf[:])
            if n % 2 == 1 or n == 6:
                nc.vector.tensor_copy(out=kT_sb[n][:], in_=kT_ps[:].rearrange("d t p -> d (t p)"))
            else:
                nc.scalar.copy(out=kT_sb[n][:], in_=kT_ps[:].rearrange("d t p -> d (t p)"))

        def scores_and_maximum(n):
            g = n % NKV
            s_ps[n] = psum3.tile([P, M], F32, tag="s", name="s_ps")
            nc.tensor.matmul(s_ps[n][:], lhsT=qT_sb[:, g, :], rhs=kT_sb[n][:], start=True, stop=True)
            nc.vector.tensor_reduce(out=neg_max[:, n : n + 1], in_=s_ps[n][:], axis=AXIS.X, op=ALU.max, negate=True)

        def exponentials(n):
            nc.scalar.activation(
                out=e_sb[n][:].rearrange("q (u p i) -> q u p i", u=2, i=2),
                in_=s_ps[n][:].rearrange("q (u i p) -> q u p i", u=2, i=2),
                func=ACT.Exp,
                bias=neg_max[:, n : n + 1],
                scale=1.0,
                accum_out=row_sum[:, n : n + 1],
            )

        def transpose_weights(n):
            eT_ps[n] = psum4.tile([P, 2, P], F32, tag="t", name="eT_ps")
            e_words = e_sb[n][:].bitcast(F32)
            for u in range(2):
                nc.tensor.transpose(eT_ps[n][:, u, :], e_words[:, u * P : (u + 1) * P], ident_f32[:])

        def group_weights(n):
            nc.scalar.copy(
                out=e_grouped[n // 2][:, n % 2 * P * PACK : (n % 2 + 1) * P * PACK].bitcast(F32).rearrange("p (q u) -> p q u", u=2),
                in_=eT_ps[n][:].rearrange("p u q -> p q u"),
            )

        def quantise_weights(n):
            codes = e_codes[:, n - 1 : n + 1, :].rearrange("p n q -> p (n q)")
            scales = e_scales[:, n - 1 : n + 1, :].rearrange("p n q -> p (n q)")
            nc.vector.quantize_mx(out=codes.bitcast(FP8X4), scales=scales, in_=e_grouped[n // 2][:])

        def regroup_values(b, c):
            cols = slice(c * 2 * HD, (c + 1) * 2 * HD)
            if b == 0:
                nc.gpsimd.tensor_scalar(
                    out=v_grouped[b][:].rearrange("p (w t) -> p w t", t=PACK)[:, cols, :],
                    in0=v_sb[b][:, :, cols].rearrange("p t w -> p w t"),
                    scalar1=1.0,
                    scalar2=0.0,
                    op0=ALU.mult,
                    op1=ALU.add,
                )
            else:
                nc.vector.tensor_copy(
                    out=v_grouped[b][:].rearrange("p (w t) -> p w t", t=PACK)[:, cols, :].rearrange("p (x i) t -> p x t i", i=4),
                    in_=v_sb[b][:, :, cols].rearrange("p t (x i) -> p x t i", i=4),
                )

        def quantise_values(b, c):
            cols = slice(c * 2 * HD, (c + 1) * 2 * HD)
            nc.vector.quantize_mx(
                out=v_codes[:, b, cols].bitcast(FP8X4),
                scales=v_scales[:, b, cols],
                in_=v_grouped[b][:, c * 2 * HD * PACK : (c + 1) * 2 * HD * PACK],
            )

        def weighted_values(n):
            b, g = divmod(n, NKV)
            c, u = divmod(g, 2)
            if u == 0:
                if b == 0:
                    o_ps[(b, c)] = psum1.tile([P, 2, HD], F32, tag="o", name="o_ps")
                    if c == 0:
                        stream_zeros(o_ps[(b, c)][:, 0, :], 8)
                else:
                    o_ps[(b, c)] = psum3.tile([P, 2, HD], F32, tag="s", name="o_ps")
            nc.tensor.matmul_mx(
                out=o_ps[(b, c)][:, u, :],
                lhsT=e_codes[:, n, :].bitcast(FP8X4),
                lhsT_scale=e_scales[:, n, :],
                rhs=v_codes[:, b, g * HD : (g + 1) * HD].bitcast(FP8X4),
                rhs_scale=v_scales[:, b, g * HD : (g + 1) * HD],
                start=True,
                stop=True,
            )

        def invert_sums(n):
            nc.vector.reciprocal(out=inv_sum[:, n - 1 : n + 1], in_=row_sum[:, n - 1 : n + 1])

        def normalise(n):
            b, g = divmod(n, NKV)
            c, u = divmod(g, 2)
            nc.vector.tensor_tensor(
                out=a_sb[b * PAIRS + c][:].rearrange("q (u d) -> q u d", u=2),
                in0=o_ps[(b, c)][:],
                in1=inv_sum[:, n - 1 : n + 1].unsqueeze(2).to_broadcast([P, 2, HD]),
                op=ALU.mult,
            )

        def transpose_heads(b, c):
            aT_ps = psum4.tile([P, P], F32, tag="t")
            nc.tensor.transpose(aT_ps[:], a_sb[b * PAIRS + c][:].bitcast(F32), ident_f32[:])
            nc.scalar.copy(
                out=a_grouped[c][:].bitcast(F32).rearrange("p (b e j) -> p b e j", b=B, j=G)[:, b],
                in_=aT_ps[:].rearrange("p (j e) -> p e j", j=G),
            )

        def quantise_heads(c):
            nc.vector.quantize_mx(out=a_codes[:, c, :].bitcast(FP8X4), scales=a_scales[:, c, :], in_=a_grouped[c][:])

        def transpose_projection(c, half):
            wT_ps[(c, half)] = psum4.tile([P, G, 2, P], F32, tag="t", name="wT_ps")
            wo_words = wo_sb[:].rearrange("p r c j u d -> p (r c j u d)").bitcast(F32)
            wo_words = wo_words.rearrange("p (r c j w) -> p r c j w", r=D // P, c=PAIRS, j=G)
            for j in range(G):
                for k in range(2):
                    nc.tensor.transpose(wT_ps[(c, half)][:, j, k, :], wo_words[:, 2 * half + k, c, j, :], ident_f32[:])

        def group_projection(c, half):
            rows = slice(half * 2 * P, (half + 1) * 2 * P)
            nc.scalar.copy(
                out=w_grouped[c][:].bitcast(F32).rearrange("p (n j) -> p n j", j=G)[:, rows, :],
                in_=wT_ps[(c, half)][:].rearrange("p j k n -> p (k n) j"),
            )

        def quantise_projection(c, half):
            rows = slice(half * 2 * P, (half + 1) * 2 * P)
            nc.vector.quantize_mx(
                out=w_codes[:, c, rows].bitcast(FP8X4),
                scales=w_scales[:, c, rows],
                in_=w_grouped[c][:, half * 2 * P * PACK : (half + 1) * 2 * P * PACK],
            )

        def project(c, half):
            cols = slice(half * D // 2, (half + 1) * D // 2)
            if half not in out_ps:
                out_ps[half] = psum3.tile([P, D], F32, tag="s", name="out_ps")
            nc.tensor.matmul_mx(
                out=out_ps[half][:, : D // 2],
                lhsT=a_codes[:, c, :].bitcast(FP8X4),
                lhsT_scale=a_scales[:, c, :],
                rhs=w_codes[:, c, cols].bitcast(FP8X4),
                rhs_scale=w_scales[:, c, cols],
                start=(c == 0),
                stop=(c == PAIRS - 1),
            )

        def store(half):
            out_rows = out.rearrange("b e n -> (b e) n")
            cols = slice(half * D // 2, (half + 1) * D // 2)
            if half == 0:
                nc.scalar.copy(out=out_sb[:, cols], in_=out_ps[half][:, : D // 2])
            else:
                nc.vector.tensor_copy(out=out_sb[:, cols], in_=out_ps[half][:, : D // 2])
            nc.sync.dma_start(out=out_rows[:, cols], in_=out_sb[:, cols])

        def unit(n):
            return 0 <= n < UNITS

        head_ps = psum1.tile([P, P], F32, tag="o", name="head_ps")
        stream_zeros(head_ps, 11)
        transpose_queries()
        transpose_keys(0)
        transpose_keys(1)
        stream_zeros(head_ps, 6)
        scores_and_maximum(0)
        transpose_keys(2)
        scores_and_maximum(1)
        transpose_keys(3)
        transpose_keys(4)
        for c in range(PAIRS):
            regroup_values(0, c)
        for r in range(UNITS):
            exponentials(r)
            if r == 0:
                scores_and_maximum(2)
                transpose_keys(5)
                transpose_keys(6)
            if r == 1:
                stream_zeros(head_ps, 5)
                scores_and_maximum(3)
                transpose_weights(0)
                transpose_keys(7)
            if r >= 2:
                if r + 2 < UNITS:
                    stream_zeros(head_ps, (0, 0, 0, 0, 0, 1)[r])
                    scores_and_maximum(r + 2)
                transpose_weights(r - 1)
                group_weights(r - 2)
            if r == 3:
                regroup_values(1, 0)
            if r == 4:
                quantise_values(0, 0)
                quantise_weights(1)
                invert_sums(1)
            if r == 5:
                quantise_values(0, 1)
            if r == 6:
                weighted_values(0)
                weighted_values(1)
                quantise_weights(3)
                invert_sums(3)
                normalise(1)
                quantise_values(1, 0)
        out_ps[0] = psum3.tile([P, D], F32, tag="s", name="out_ps")
        transpose_projection(0, 0)
        group_projection(0, 0)
        stream_values(out_ps[0][:], 1)
        transpose_weights(7)
        stream_values(out_ps[0][:], 1)
        weighted_values(2)
        weighted_values(3)
        regroup_values(1, 1)
        quantise_weights(5)
        invert_sums(5)
        normalise(3)
        group_weights(6)
        group_weights(7)
        transpose_projection(0, 1)
        group_projection(0, 1)
        transpose_projection(1, 0)
        group_projection(1, 0)
        weighted_values(4)
        weighted_values(5)
        quantise_values(1, 1)
        quantise_weights(7)
        invert_sums(7)
        normalise(5)
        transpose_projection(1, 1)
        group_projection(1, 1)
        stream_values(out_ps[0][:], 1)
        weighted_values(6)
        weighted_values(7)
        transpose_heads(0, 0)
        transpose_heads(0, 1)
        quantise_projection(0, 0)
        normalise(7)
        transpose_heads(1, 0)
        quantise_projection(0, 1)
        quantise_projection(1, 0)
        quantise_heads(0)
        transpose_heads(1, 1)
        quantise_projection(1, 1)
        stream_values(out_ps[0][:], 2)
        project(0, 0)
        project(0, 1)
        quantise_heads(1)
        project(1, 0)
        project(1, 1)
        store(0)
        store(1)
